import numpy as np
import ml_dtypes


def mxq(x, axis, fmt="e4m3"):
    dtype, down = {"e4m3": (ml_dtypes.float8_e4m3fn, 7), "e5m2": (ml_dtypes.float8_e5m2, 14)}[fmt]
    v = np.moveaxis(np.asarray(x, np.float32).astype(ml_dtypes.bfloat16).astype(np.float64), axis, -1)
    blocks = v.reshape(v.shape[:-1] + (-1, 32))
    amax = np.abs(blocks).max(-1, keepdims=True)
    byte = np.maximum(np.where(amax > 0, np.frexp(amax)[1] - 1 + 127, 0) - down, 1)
    scale = np.exp2(byte - 127.0)
    codes = (blocks / scale).astype(np.float32).astype(dtype).astype(np.float64)
    return np.moveaxis((codes * scale).reshape(v.shape), -1, axis)


WIDE = False


def mx_kscale(k):
    if not WIDE:
        return np.ones(k)
    levels = np.array([10, -10, 5, -5, 0])
    a = np.random.permutation(np.resize(levels, k // 512 * 4)).reshape(k // 512, 4)
    idx = np.arange(k)
    return np.exp2(a[idx // 512, idx % 128 // 32])


BF16 = ml_dtypes.bfloat16


def bf(x):
    return np.asarray(x, np.float32).astype(BF16)


def f64(x):
    return np.asarray(x).astype(np.float64)


E2M1 = np.array([0.0, 0.5, 1.0, 1.5, 2.0, 3.0, 4.0, 6.0, -0.0, -0.5, -1.0, -1.5, -2.0, -3.0, -4.0, -6.0])


def pack_weight(w, fmt):
    k, n = w.shape
    w = f64(bf(w)).reshape(k // 32, 32, n)
    amax = np.abs(w).max(1)
    if fmt == "e4m3":
        byte = np.frexp(amax)[1] - 1 + 127 - 7
    else:
        mant, ex = np.frexp(amax / 6.0)
        byte = np.where(mant > 0.5, ex, ex - 1) + 127
    byte = np.clip(np.where(amax > 0, byte, 1), 1, 254)
    scaled = (w * np.exp2(127.0 - byte)[:, None, :]).reshape(k, n).astype(np.float32)
    by_word = np.ascontiguousarray(scaled.reshape(k // 512, 128, 4, n).transpose(0, 1, 3, 2))
    if fmt == "e4m3":
        words = by_word.astype(ml_dtypes.float8_e4m3fn).view(np.uint8)
    else:
        c = by_word.astype(ml_dtypes.float4_e2m1fn).view(np.uint8) & 0xF
        words = c[..., 0::2] | (c[..., 1::2] << 4)
    return np.ascontiguousarray(words), np.ascontiguousarray(byte.astype(np.uint8).reshape(k // 512, 16, n))


def unpack_weight(words, scales, fmt):
    g, p, n, _ = words.shape
    if fmt == "e4m3":
        vals = np.ascontiguousarray(words).view(ml_dtypes.float8_e4m3fn).astype(np.float64)
    else:
        nib = np.empty((g, p, n, 4), np.uint8)
        nib[..., 0::2] = words & 0xF
        nib[..., 1::2] = words >> 4
        vals = E2M1[nib]
    vals = vals * np.repeat(np.exp2(scales.astype(np.float64) - 127.0), 8, axis=1)[..., None]
    return vals.transpose(0, 1, 3, 2).reshape(g * 512, n)

def pack4(w):
    words, scales = pack_weight(w, "e2m1")
    return words.reshape(words.shape[0], 128, -1), scales


def unpack4(words, scales):
    return unpack_weight(words.reshape(words.shape[0], 128, -1, 2), scales, "e2m1")


B, S, D_IN, D_OUT = 4, 2048, 512, 512


def setup_inputs():
    s = mx_kscale(D_IN)
    x = bf(np.random.standard_normal((B, S, D_IN)) * s)
    weight = np.random.standard_normal((D_OUT, D_IN)) * 0.04 / s[None, :]
    words, scales = pack4(np.ascontiguousarray(weight.T))
    return {"x": x, "weight_words": words, "weight_scales": scales}


def reference(x, weight_words, weight_scales):
    wq = unpack4(weight_words, weight_scales).T
    x2 = f64(x).reshape(-1, D_IN)
    xq = mxq(x2, 1, "e4m3")
    out2 = xq @ wq.T
    return out2.reshape(B, S, D_OUT)

@@ -1,0 +1,132 @@
+from contextlib import ExitStack
+
+import concourse.mybir as mybir
+from concourse.masks import make_identity
+
+BF16 = mybir.dt.bfloat16
+F32 = mybir.dt.float32
+I32 = mybir.dt.int32
+U8 = mybir.dt.uint8
+U32 = mybir.dt.uint32
+FP8X4 = mybir.dt.float8_e4m3fn_x4
+FP4X4 = mybir.dt.float4_e2m1fn_x4
+
+P = 128
+ROWS = 8192
+K = 512
+N = 512
+NT = ROWS // P
+
+FLOPS = 2 * ROWS * K * N
+
+MANUAL = True
+LOAD_CHUNKS = [4, 4, 8, 16, 16, 16]
+STORE_TILES = 8
+UNIT = 2
+GROUP = 2
+
+
+def tile_fp8purelinear_kernel(tc, x, weight_words, weight_scales, out):
+    nc = tc.nc
+    xv = x.flatten_outer_dims().rearrange("(p j) k -> p j k", j=NT)
+    ov = out.flatten_outer_dims().rearrange("(p j) n -> p j n", j=NT)
+
+    with ExitStack() as ctx:
+        const = ctx.enter_context(tc.tile_pool(name="const", bufs=1))
+        xin = ctx.enter_context(tc.tile_pool(name="xin", bufs=1))
+        res = ctx.enter_context(tc.tile_pool(name="res", bufs=1))
+        stage = ctx.enter_context(tc.tile_pool(name="stage", bufs=4))
+        ps_t = ctx.enter_context(tc.psum_pool(name="ps_t", bufs=4))
+        ps_o = ctx.enter_context(tc.psum_pool(name="ps_o", bufs=4))
+        if MANUAL:
+            ctx.enter_context(tc.manual_schedule())
+
+        w_words = const.tile([P, 2 * N], U8, name="w_words", align_bytes=64)
+        w_plane = const.tile([P, N], U8, name="w_plane", align_bytes=64)
+        ident = const.tile([P, P], F32, name="ident")
+
+        nc.vector.memset(w_plane[:].bitcast(I32), 0)
+        make_identity(nc, ident[:])
+
+        x_of = {}
+        j0 = 0
+        for c, width in enumerate(LOAD_CHUNKS):
+            xt = xin.tile([P, width, K], BF16, name="x%d" % c)
+            nc.sync.dma_start(out=xt[:], in_=xv[:, j0 : j0 + width, :])
+            for i in range(width):
+                x_of[j0 + i] = (xt, i)
+            j0 += width
+            if c == 0:
+                nc.sync.dma_start(out=w_words[:].bitcast(I32), in_=weight_words[0].bitcast(I32))
+                for r in range(4):
+                    nc.sync.dma_start(
+                        out=w_plane[r:P:32, :].bitcast(I32),
+                        in_=weight_scales[0, r:16:4, :].bitcast(I32),
+                    )
+        assert j0 == NT
+
+        banks = {}
+        grouped = {}
+        codes = {}
+        planes = {}
+        o_tiles = {}
+
+        def transposes(h):
+            tp = ps_t.tile([P, UNIT, 2, P], F32, name="tp")
+            banks[h] = tp
+            for a in range(UNIT):
+                xt, i = x_of[UNIT * h + a]
+                words = xt[:, i, :].bitcast(F32)
+                for u in range(2):
+                    nc.tensor.transpose(tp[:, a, u, :], words[:, u : K // 2 : 2], ident[:])
+
+        def regroup(h):
+            gr = stage.tile([P, UNIT * P * 4], BF16, name="gr", align_bytes=64)
+            grouped[h] = gr
+            nc.vector.tensor_copy(
+                out=gr[:].bitcast(F32).rearrange("p (a r u) -> p a r u", a=UNIT, u=2),
+                in_=banks[h][:].rearrange("p a u r -> p a r u"),
+            )
+
+        def quantise(h):
+            cd = stage.tile([P, UNIT * P], U32, name="cd", align_bytes=64)
+            pl = stage.tile([P, UNIT * P], U8, name="pl", align_bytes=64)
+            codes[h] = cd
+            planes[h] = pl
+            nc.vector.quantize_mx(out=cd[:].bitcast(FP8X4), scales=pl[:], in_=grouped[h][:])
+
+        def passes(h):
+            for a in range(UNIT):
+                j = UNIT * h + a
+                s, jj = divmod(j, STORE_TILES)
+                if jj == 0:
+                    o_tiles[s] = res.tile([P, STORE_TILES, N], F32, name="o%d" % s)
+                acc = ps_o.tile([P, N], F32, name="acc")
+                nc.tensor.matmul_mx(
+                    out=acc[:],
+                    lhsT=codes[h][:, a * P : (a + 1) * P].bitcast(FP8X4),
+                    lhsT_scale=planes[h][:, a * P : (a + 1) * P],
+                    rhs=w_words[:].bitcast(FP4X4),
+                    rhs_scale=w_plane[:],
+                    start=True,
+                    stop=True,
+                )
+                nc.scalar.copy(out=o_tiles[s][:, jj, :], in_=acc[:])
+                if jj == STORE_TILES - 1:
+                    nc.sync.dma_start(
+                        out=ov[:, s * STORE_TILES : (s + 1) * STORE_TILES, :], in_=o_tiles[s][:]
+                    )
+
+        n_groups = NT // (UNIT * GROUP)
+        for g in range(n_groups + 1):
+            if g < n_groups:
+                hs = [GROUP * g + i for i in range(GROUP)]
+                for h in hs:
+                    transposes(h)
+                for h in hs:
+                    regroup(h)
+                for h in hs:
+                    quantise(h)
+            if g >= 1:
+                for i in range(GROUP):
+                    passes(GROUP * (g - 1) + i)

@@ -20,8 +20,8 @@ NT = ROWS // P
 FLOPS = 2 * ROWS * K * N
 
 MANUAL = True
-LOAD_CHUNKS = [4, 4, 8, 16, 16, 16]
-STORE_TILES = 8
+LOAD_CHUNKS = [4, 12, 16, 32]
+STORE_CHUNKS = [16, 16, 16, 8, 8]
 UNIT = 2
 GROUP = 2
 
@@ -70,6 +70,13 @@ def tile_fp8purelinear_kernel(tc, x, weight_words, weight_scales, out):
         codes = {}
         planes = {}
         o_tiles = {}
+        o_of = {}
+        j0 = 0
+        for s, width in enumerate(STORE_CHUNKS):
+            for i in range(width):
+                o_of[j0 + i] = (s, i, width, j0)
+            j0 += width
+        assert j0 == NT
 
         def transposes(h):
             tp = ps_t.tile([P, UNIT, 2, P], F32, name="tp")
@@ -98,9 +105,9 @@ def tile_fp8purelinear_kernel(tc, x, weight_words, weight_scales, out):
         def passes(h):
             for a in range(UNIT):
                 j = UNIT * h + a
-                s, jj = divmod(j, STORE_TILES)
+                s, jj, width, first = o_of[j]
                 if jj == 0:
-                    o_tiles[s] = res.tile([P, STORE_TILES, N], F32, name="o%d" % s)
+                    o_tiles[s] = res.tile([P, width, N], F32, name="o%d" % s)
                 acc = ps_o.tile([P, N], F32, name="acc")
                 nc.tensor.matmul_mx(
                     out=acc[:],
@@ -112,10 +119,8 @@ def tile_fp8purelinear_kernel(tc, x, weight_words, weight_scales, out):
                     stop=True,
                 )
                 nc.scalar.copy(out=o_tiles[s][:, jj, :], in_=acc[:])
-                if jj == STORE_TILES - 1:
-                    nc.sync.dma_start(
-                        out=ov[:, s * STORE_TILES : (s + 1) * STORE_TILES, :], in_=o_tiles[s][:]
-                    )
+                if jj == width - 1:
+                    nc.sync.dma_start(out=ov[:, first : first + width, :], in_=o_tiles[s][:])
 
         n_groups = NT // (UNIT * GROUP)
         for g in range(n_groups + 1):

@@ -20,7 +20,7 @@ NT = ROWS // P
 FLOPS = 2 * ROWS * K * N
 
 MANUAL = True
-LOAD_CHUNKS = [4, 12, 16, 32]
+LOAD_CHUNKS = [4, 8, 20, 32]
 STORE_CHUNKS = [16, 16, 16, 8, 8]
 UNIT = 2
 GROUP = 2
@@ -56,7 +56,7 @@ def tile_fp8purelinear_kernel(tc, x, weight_words, weight_scales, out):
             for i in range(width):
                 x_of[j0 + i] = (xt, i)
             j0 += width
-            if c == 0:
+            if c == 1:
                 nc.sync.dma_start(out=w_words[:].bitcast(I32), in_=weight_words[0].bitcast(I32))
                 for r in range(4):
                     nc.sync.dma_start(

@@ -19,8 +19,8 @@ NT = ROWS // P
 
 FLOPS = 2 * ROWS * K * N
 
-MANUAL = True
-LOAD_CHUNKS = [4, 8, 20, 32]
+MANUAL = False
+LOAD_CHUNKS = [4, 12, 16, 32]
 STORE_CHUNKS = [16, 16, 16, 8, 8]
 UNIT = 2
 GROUP = 2
@@ -56,7 +56,7 @@ def tile_fp8purelinear_kernel(tc, x, weight_words, weight_scales, out):
             for i in range(width):
                 x_of[j0 + i] = (xt, i)
             j0 += width
-            if c == 1:
+            if c == 0:
                 nc.sync.dma_start(out=w_words[:].bitcast(I32), in_=weight_words[0].bitcast(I32))
                 for r in range(4):
                     nc.sync.dma_start(

from contextlib import ExitStack

import concourse.mybir as mybir
from concourse.masks import make_identity

BF16 = mybir.dt.bfloat16
F32 = mybir.dt.float32
I32 = mybir.dt.int32
U8 = mybir.dt.uint8
U32 = mybir.dt.uint32
FP8X4 = mybir.dt.float8_e4m3fn_x4
FP4X4 = mybir.dt.float4_e2m1fn_x4

P = 128
ROWS = 8192
K = 512
N = 512
NT = ROWS // P

FLOPS = 2 * ROWS * K * N

MANUAL = False
LOAD_CHUNKS = [4, 12, 16, 32]
STORE_CHUNKS = [16, 16, 16, 8, 8]
UNIT = 2
GROUP = 2


def tile_fp8purelinear_kernel(tc, x, weight_words, weight_scales, out):
    nc = tc.nc
    xv = x.flatten_outer_dims().rearrange("(p j) k -> p j k", j=NT)
    ov = out.flatten_outer_dims().rearrange("(p j) n -> p j n", j=NT)

    with ExitStack() as ctx:
        const = ctx.enter_context(tc.tile_pool(name="const", bufs=1))
        xin = ctx.enter_context(tc.tile_pool(name="xin", bufs=1))
        res = ctx.enter_context(tc.tile_pool(name="res", bufs=1))
        stage = ctx.enter_context(tc.tile_pool(name="stage", bufs=4))
        ps_t = ctx.enter_context(tc.psum_pool(name="ps_t", bufs=4))
        ps_o = ctx.enter_context(tc.psum_pool(name="ps_o", bufs=4))
        if MANUAL:
            ctx.enter_context(tc.manual_schedule())

        w_words = const.tile([P, 2 * N], U8, name="w_words", align_bytes=64)
        w_plane = const.tile([P, N], U8, name="w_plane", align_bytes=64)
        ident = const.tile([P, P], F32, name="ident")

        nc.vector.memset(w_plane[:].bitcast(I32), 0)
        make_identity(nc, ident[:])

        x_of = {}
        j0 = 0
        for c, width in enumerate(LOAD_CHUNKS):
            xt = xin.tile([P, width, K], BF16, name="x%d" % c)
            nc.sync.dma_start(out=xt[:], in_=xv[:, j0 : j0 + width, :])
            for i in range(width):
                x_of[j0 + i] = (xt, i)
            j0 += width
            if c == 0:
                nc.sync.dma_start(out=w_words[:].bitcast(I32), in_=weight_words[0].bitcast(I32))
                for r in range(4):
                    nc.sync.dma_start(
                        out=w_plane[r:P:32, :].bitcast(I32),
                        in_=weight_scales[0, r:16:4, :].bitcast(I32),
                    )
        assert j0 == NT

        banks = {}
        grouped = {}
        codes = {}
        planes = {}
        o_tiles = {}
        o_of = {}
        j0 = 0
        for s, width in enumerate(STORE_CHUNKS):
            for i in range(width):
                o_of[j0 + i] = (s, i, width, j0)
            j0 += width
        assert j0 == NT

        def transposes(h):
            tp = ps_t.tile([P, UNIT, 2, P], F32, name="tp")
            banks[h] = tp
            for a in range(UNIT):
                xt, i = x_of[UNIT * h + a]
                words = xt[:, i, :].bitcast(F32)
                for u in range(2):
                    nc.tensor.transpose(tp[:, a, u, :], words[:, u : K // 2 : 2], ident[:])

        def regroup(h):
            gr = stage.tile([P, UNIT * P * 4], BF16, name="gr", align_bytes=64)
            grouped[h] = gr
            nc.vector.tensor_copy(
                out=gr[:].bitcast(F32).rearrange("p (a r u) -> p a r u", a=UNIT, u=2),
                in_=banks[h][:].rearrange("p a u r -> p a r u"),
            )

        def quantise(h):
            cd = stage.tile([P, UNIT * P], U32, name="cd", align_bytes=64)
            pl = stage.tile([P, UNIT * P], U8, name="pl", align_bytes=64)
            codes[h] = cd
            planes[h] = pl
            nc.vector.quantize_mx(out=cd[:].bitcast(FP8X4), scales=pl[:], in_=grouped[h][:])

        def passes(h):
            for a in range(UNIT):
                j = UNIT * h + a
                s, jj, width, first = o_of[j]
                if jj == 0:
                    o_tiles[s] = res.tile([P, width, N], F32, name="o%d" % s)
                acc = ps_o.tile([P, N], F32, name="acc")
                nc.tensor.matmul_mx(
                    out=acc[:],
                    lhsT=codes[h][:, a * P : (a + 1) * P].bitcast(FP8X4),
                    lhsT_scale=planes[h][:, a * P : (a + 1) * P],
                    rhs=w_words[:].bitcast(FP4X4),
                    rhs_scale=w_plane[:],
                    start=True,
                    stop=True,
                )
                nc.scalar.copy(out=o_tiles[s][:, jj, :], in_=acc[:])
                if jj == width - 1:
                    nc.sync.dma_start(out=ov[:, first : first + width, :], in_=o_tiles[s][:])

        n_groups = NT // (UNIT * GROUP)
        for g in range(n_groups + 1):
            if g < n_groups:
                hs = [GROUP * g + i for i in range(GROUP)]
                for h in hs:
                    transposes(h)
                for h in hs:
                    regroup(h)
                for h in hs:
                    quantise(h)
            if g >= 1:
                for i in range(GROUP):
                    passes(GROUP * (g - 1) + i)
